import numpy as np
import ml_dtypes


def mxq(x, axis, fmt="e4m3"):
    dtype, down = {"e4m3": (ml_dtypes.float8_e4m3fn, 7), "e5m2": (ml_dtypes.float8_e5m2, 14)}[fmt]
    v = np.moveaxis(np.asarray(x, np.float32).astype(ml_dtypes.bfloat16).astype(np.float64), axis, -1)
    blocks = v.reshape(v.shape[:-1] + (-1, 32))
    amax = np.abs(blocks).max(-1, keepdims=True)
    byte = np.maximum(np.where(amax > 0, np.frexp(amax)[1] - 1 + 127, 0) - down, 1)
    scale = np.exp2(byte - 127.0)
    codes = (blocks / scale).astype(np.float32).astype(dtype).astype(np.float64)
    return np.moveaxis((codes * scale).reshape(v.shape), -1, axis)


WIDE = False


def mx_kscale(k):
    if not WIDE:
        return np.ones(k)
    levels = np.array([20, -20, 10, -10, 0])
    a = np.random.permutation(np.resize(levels, k // 512 * 4)).reshape(k // 512, 4)
    idx = np.arange(k)
    return np.exp2(a[idx // 512, idx % 128 // 32])


BF16 = ml_dtypes.bfloat16


def bf(x):
    return np.asarray(x, np.float32).astype(BF16)


def f64(x):
    return np.asarray(x).astype(np.float64)


B, S, DIM, H, NOPE, ROPE, VHD, KV_RANK = 2, 256, 2048, 16, 128, 64, 128, 512
QKHD = NOPE + ROPE
HALF = ROPE // 2


def rope(u, cos, sin):
    ur = u.reshape(u.shape[:-1] + (HALF, 2))
    a, b = ur[..., 0], ur[..., 1]
    c = cos[None, :, None, :]
    s = sin[None, :, None, :]
    return np.stack([a * c - b * s, a * s + b * c], axis=-1).reshape(u.shape)


def setup_inputs():
    u = np.repeat(mx_kscale(H * QKHD)[0::2], 2)
    inv_freq = 1.0 / 10000.0 ** (np.arange(0, ROPE, 2) / ROPE)
    ang = np.arange(S)[:, None] * inv_freq[None, :]
    x = np.random.standard_normal((B, S, DIM))
    wq_w = np.random.standard_normal((DIM, H * QKHD)) / np.sqrt(DIM) / u[None, :]
    wq_b = np.random.standard_normal(H * QKHD) * 0.2
    g = np.random.standard_normal((B, S, H, QKHD)) * np.exp2(np.random.randint(-12, 1, (B, S, 1, 1))) * 4.0
    g = g * u.reshape(H, QKHD)[None, None, :, :]
    return {"x": bf(x), "wq_w": bf(wq_w), "wq_b": bf(wq_b),
            "cos": bf(np.cos(ang)), "sin": bf(np.sin(ang)), "grad_out": bf(g)}


def reference(x, wq_w, wq_b, cos, sin, grad_out):
    g = f64(grad_out)
    gq = np.concatenate([g[..., :NOPE], rope(g[..., NOPE:], f64(cos), -f64(sin))], axis=-1)
    gq = gq.reshape(B, S, H * QKHD)
    return mxq(gq, 2, "e5m2") @ mxq(f64(wq_w), 1, "e4m3").T

@@ -1,0 +1,244 @@
+from contextlib import ExitStack
+
+import concourse.mybir as mybir
+from concourse.masks import make_identity
+
+F32 = mybir.dt.float32
+BF16 = mybir.dt.bfloat16
+U32 = mybir.dt.uint32
+U8 = mybir.dt.uint8
+E4M3_X4 = mybir.dt.float8_e4m3fn_x4
+E5M2_X4 = mybir.dt.float8_e5m2_x4
+MULT = mybir.AluOpType.mult
+ADD = mybir.AluOpType.add
+
+P = 128
+TOKENS = 512
+DIM = 2048
+HEADS = 16
+HEAD = 192
+NOPE = 128
+PAIRS = 32
+K = HEADS * HEAD
+
+PASS_WORDS = 256
+PASSES = K // (2 * PASS_WORDS)
+CHUNK = 512
+CHUNKS = DIM // CHUNK
+CHUNK_TILES = CHUNK // P
+UNIT_PASSES = 2
+CHUNK_UNITS = PASSES // UNIT_PASSES
+UNITS = CHUNKS * CHUNK_UNITS
+UNIT_K = UNIT_PASSES * 2 * PASS_WORDS
+HALF_TILES = 2
+BANK_ROWS = 2 * P
+RAW_UNITS = 8
+ROPE_HEADS = 4
+
+FLOPS = 2 * TOKENS * DIM * K
+BYTES = 2 * DIM * K + 2 * TOKENS * K + 4 * TOKENS * DIM + 2 * 2 * 256 * PAIRS
+
+
+def tile_mla_pb_kernel(tc, x, wq_w, wq_b, cos, sin, grad_out, out):
+    nc = tc.nc
+    g_rows = grad_out.rearrange("b s h e -> (b s) (h e)")
+    out_rows = out.rearrange("b s d -> (b s) d")
+
+    with ExitStack() as ctx:
+        ctx.enter_context(tc.manual_schedule())
+        const = ctx.enter_context(tc.tile_pool(name="const", bufs=1))
+        raw = ctx.enter_context(tc.tile_pool(name="raw", bufs=RAW_UNITS))
+        packed = ctx.enter_context(tc.tile_pool(name="packed", bufs=1))
+        stage = ctx.enter_context(tc.tile_pool(name="stage", bufs=8))
+        products = ctx.enter_context(tc.tile_pool(name="products", bufs=2))
+        results = ctx.enter_context(tc.tile_pool(name="results", bufs=8))
+        turned = ctx.enter_context(tc.psum_pool(name="turned", bufs=4))
+        sums = ctx.enter_context(tc.psum_pool(name="sums", bufs=4))
+
+        ident = const.tile([P, P], F32)
+        make_identity(nc, ident[:])
+        cos_sb = const.tile([P, 2, PAIRS], BF16)
+        sin_sb = const.tile([P, 2, PAIRS], BF16)
+        nc.scalar.dma_start(out=cos_sb[:], in_=cos.rearrange("(s p) j -> p s j", p=P))
+        nc.scalar.dma_start(out=sin_sb[:], in_=sin.rearrange("(s p) j -> p s j", p=P))
+        neg_sin = const.tile([P, 2, PAIRS], BF16)
+        nc.vector.tensor_scalar_mul(out=neg_sin[:], in0=sin_sb[:], scalar1=-1.0)
+
+        g_tiles = [const.tile([P, K], BF16, name="g%d" % t) for t in range(TOKENS // P)]
+        w_units = {}
+
+        def load_tokens(t):
+            nc.sync.dma_start(out=g_tiles[t][:], in_=g_rows[t * P : (t + 1) * P, :])
+
+        def load_unit(n):
+            c, r = divmod(n, CHUNK_UNITS)
+            w_units[n] = raw.tile([P, CHUNK_TILES, UNIT_K], BF16, name="w_unit", tag="w_unit")
+            nc.sync.dma_start(
+                out=w_units[n][:],
+                in_=wq_w[c * CHUNK : (c + 1) * CHUNK, r * UNIT_K : (r + 1) * UNIT_K].rearrange(
+                    "(i p) k -> p i k", p=P
+                ),
+            )
+
+        load_tokens(0)
+        load_tokens(1)
+        load_unit(0)
+        load_unit(1)
+        load_tokens(2)
+        load_tokens(3)
+        for n in range(2, RAW_UNITS):
+            load_unit(n)
+
+        def rotate(t, first_head, heads):
+            s = t % 2
+            pairs = g_tiles[t][:].rearrange("p (h e) -> p h e", e=HEAD)[
+                :, first_head : first_head + heads, NOPE:HEAD
+            ].rearrange("p h (j e) -> p h j e", e=2)
+            by_cos = products.tile([P, heads, PAIRS, 2], F32, tag="by_cos")
+            by_sin = products.tile([P, 2, heads, PAIRS], F32, tag="by_sin")
+            nc.vector.tensor_tensor(
+                out=by_cos[:],
+                in0=pairs,
+                in1=cos_sb[:, s, :].unsqueeze(1).unsqueeze(3).to_broadcast([P, heads, PAIRS, 2]),
+                op=MULT,
+            )
+            nc.vector.tensor_tensor(
+                out=by_sin[:, 0],
+                in0=pairs[:, :, :, 1],
+                in1=sin_sb[:, s, :].unsqueeze(1).to_broadcast([P, heads, PAIRS]),
+                op=MULT,
+            )
+            nc.vector.tensor_tensor(
+                out=by_sin[:, 1],
+                in0=pairs[:, :, :, 0],
+                in1=neg_sin[:, s, :].unsqueeze(1).to_broadcast([P, heads, PAIRS]),
+                op=MULT,
+            )
+            nc.vector.tensor_tensor(
+                out=pairs, in0=by_cos[:], in1=by_sin[:].rearrange("p e h j -> p h j e"), op=ADD
+            )
+
+        def pack_bank(row_words, codes, scales, fp8_x4):
+            bank = turned.tile([P, 2, BANK_ROWS], F32, tag="bank")
+            for i, words in enumerate(row_words):
+                for u in range(2):
+                    nc.tensor.transpose(
+                        bank[:, u, i * P : (i + 1) * P], words[:, u * P : (u + 1) * P], ident[:]
+                    )
+            grouped = stage.tile([P, 4 * BANK_ROWS], BF16, tag="grouped", align_bytes=64)
+            nc.scalar.copy(
+                out=grouped[:].bitcast(F32).rearrange("p (r u) -> p r u", u=2),
+                in_=bank[:].rearrange("p u r -> p r u"),
+            )
+            nc.vector.quantize_mx(out=codes.bitcast(fp8_x4), scales=scales, in_=grouped[:])
+
+        gq_codes = {}
+        gq_scales = {}
+
+        def pack_tokens(half, r):
+            gq_codes[half, r] = packed.tile(
+                [P, UNIT_PASSES, BANK_ROWS], U32, name="gq_codes%d%d" % (half, r), align_bytes=64
+            )
+            gq_scales[half, r] = packed.tile(
+                [P, UNIT_PASSES, BANK_ROWS], U8, name="gq_scales%d%d" % (half, r), align_bytes=64
+            )
+            for j in range(UNIT_PASSES):
+                first = (r * UNIT_PASSES + j) * PASS_WORDS
+                pack_bank(
+                    [
+                        g_tiles[half * HALF_TILES + i][:].bitcast(F32)[:, first : first + PASS_WORDS]
+                        for i in range(HALF_TILES)
+                    ],
+                    gq_codes[half, r][:, j, :],
+                    gq_scales[half, r][:, j, :],
+                    E5M2_X4,
+                )
+
+        w_codes = {}
+        w_scales = {}
+
+        def pack_unit(n):
+            w_codes[n] = packed.tile(
+                [P, UNIT_PASSES, CHUNK], U32, name="w_codes%d" % n, align_bytes=64
+            )
+            w_scales[n] = packed.tile(
+                [P, UNIT_PASSES, CHUNK], U8, name="w_scales%d" % n, align_bytes=64
+            )
+            words = w_units[n][:].bitcast(F32)
+            for j in range(UNIT_PASSES):
+                for b in range(CHUNK // BANK_ROWS):
+                    cols = slice(b * BANK_ROWS, (b + 1) * BANK_ROWS)
+                    pack_bank(
+                        [
+                            words[:, 2 * b + i, j * PASS_WORDS : (j + 1) * PASS_WORDS]
+                            for i in range(2)
+                        ],
+                        w_codes[n][:, j, cols],
+                        w_scales[n][:, j, cols],
+                        E4M3_X4,
+                    )
+
+        def multiply(acc, half, i, n, j):
+            r = n % CHUNK_UNITS
+            nc.tensor.matmul_mx(
+                out=acc[:],
+                lhsT=gq_codes[half, r][:, j, i * P : (i + 1) * P].bitcast(E5M2_X4),
+                lhsT_scale=gq_scales[half, r][:, j, i * P : (i + 1) * P],
+                rhs=w_codes[n][:, j, :].bitcast(E4M3_X4),
+                rhs_scale=w_scales[n][:, j, :],
+                start=(r == 0 and j == 0),
+                stop=(r == CHUNK_UNITS - 1 and j == UNIT_PASSES - 1),
+            )
+
+        def store(acc, half, i, c):
+            t = half * HALF_TILES + i
+            res = results.tile([P, CHUNK], F32, tag="res")
+            if i % 2 == 0:
+                nc.vector.tensor_copy(out=res[:], in_=acc[:])
+            else:
+                nc.scalar.copy(out=res[:], in_=acc[:])
+            nc.sync.dma_start(
+                out=out_rows[t * P : (t + 1) * P, c * CHUNK : (c + 1) * CHUNK], in_=res[:]
+            )
+
+        rotate(0, 0, HEADS)
+        rotate(1, 0, HEADS)
+        pack_unit(0)
+        pack_tokens(0, 0)
+
+        pieces = [
+            (t, h) for t in range(HALF_TILES, 2 * HALF_TILES) for h in range(0, HEADS, ROPE_HEADS)
+        ]
+        accs = []
+        for n in range(UNITS):
+            c, r = divmod(n, CHUNK_UNITS)
+            if n + RAW_UNITS < UNITS:
+                load_unit(n + RAW_UNITS)
+            if n + 1 < UNITS:
+                pack_unit(n + 1)
+            if n + 1 < CHUNK_UNITS:
+                pack_tokens(0, n + 1)
+            if n >= UNITS - CHUNK_UNITS:
+                pack_tokens(1, n - (UNITS - CHUNK_UNITS))
+            if r == 0:
+                accs = [
+                    sums.tile([P, CHUNK], F32, name="acc%d" % i, tag="acc")
+                    for i in range(HALF_TILES)
+                ]
+            for j in range(UNIT_PASSES):
+                for i in range(HALF_TILES):
+                    multiply(accs[i], 0, i, n, j)
+            if 1 <= n <= len(pieces):
+                t, h = pieces[n - 1]
+                rotate(t, h, ROPE_HEADS)
+            if r == CHUNK_UNITS - 1:
+                for i in range(HALF_TILES):
+                    store(accs[i], 0, i, c)
+
+        for c in range(CHUNKS):
+            for i in range(HALF_TILES):
+                acc = sums.tile([P, CHUNK], F32, tag="acc")
+                for n in range(c * CHUNK_UNITS, (c + 1) * CHUNK_UNITS):
+                    for j in range(UNIT_PASSES):
+                        multiply(acc, 1, i, n, j)
+                store(acc, 1, i, c)

@@ -33,7 +33,10 @@ UNIT_K = UNIT_PASSES * 2 * PASS_WORDS
 HALF_TILES = 2
 BANK_ROWS = 2 * P
 RAW_UNITS = 8
-ROPE_HEADS = 4
+UNIT_ORDER = [(c, r) for pair in (0, 2) for r in range(CHUNK_UNITS) for c in (pair, pair + 1)]
+ROPE_HEADS_OF = [
+    [h for h in range(HEADS) if (h * HEAD + NOPE) // UNIT_K == r] for r in range(CHUNK_UNITS)
+]
 
 FLOPS = 2 * TOKENS * DIM * K
 BYTES = 2 * DIM * K + 2 * TOKENS * K + 4 * TOKENS * DIM + 2 * 2 * 256 * PAIRS
@@ -67,29 +70,43 @@ def tile_mla_pb_kernel(tc, x, wq_w, wq_b, cos, sin, grad_out, out):
         g_tiles = [const.tile([P, K], BF16, name="g%d" % t) for t in range(TOKENS // P)]
         w_units = {}
 
-        def load_tokens(t):
-            nc.sync.dma_start(out=g_tiles[t][:], in_=g_rows[t * P : (t + 1) * P, :])
+        def load_tokens(t, r):
+            cols = slice(r * UNIT_K, (r + 1) * UNIT_K)
+            nc.sync.dma_start(out=g_tiles[t][:, cols], in_=g_rows[t * P : (t + 1) * P, cols])
 
-        def load_unit(n):
-            c, r = divmod(n, CHUNK_UNITS)
+        def load_unit(n, pieces=1):
+            c, r = UNIT_ORDER[n]
             w_units[n] = raw.tile([P, CHUNK_TILES, UNIT_K], BF16, name="w_unit", tag="w_unit")
-            nc.sync.dma_start(
-                out=w_units[n][:],
-                in_=wq_w[c * CHUNK : (c + 1) * CHUNK, r * UNIT_K : (r + 1) * UNIT_K].rearrange(
-                    "(i p) k -> p i k", p=P
-                ),
-            )
+            step = CHUNK_TILES // pieces
+            for i in range(0, CHUNK_TILES, step):
+                nc.sync.dma_start(
+                    out=w_units[n][:, i : i + step, :],
+                    in_=wq_w[
+                        c * CHUNK + i * P : c * CHUNK + (i + step) * P, r * UNIT_K : (r + 1) * UNIT_K
+                    ].rearrange("(i p) k -> p i k", p=P),
+                )
 
-        load_tokens(0)
-        load_tokens(1)
-        load_unit(0)
-        load_unit(1)
-        load_tokens(2)
-        load_tokens(3)
-        for n in range(2, RAW_UNITS):
-            load_unit(n)
+        load_tokens(0, 0)
+        load_tokens(1, 0)
+        load_unit(0, 2)
+        load_tokens(0, 1)
+        load_tokens(1, 1)
+        load_unit(1, 2)
+        load_unit(2)
+        load_tokens(0, 2)
+        load_tokens(1, 2)
+        load_unit(3)
+        load_unit(4)
+        for r in range(CHUNK_UNITS):
+            load_tokens(2, r)
+        load_unit(5)
+        for r in range(CHUNK_UNITS):
+            load_tokens(3, r)
+        load_unit(6)
+        load_unit(7)
 
-        def rotate(t, first_head, heads):
+        def rotate(t, r):
+            first_head, heads = ROPE_HEADS_OF[r][0], len(ROPE_HEADS_OF[r])
             s = t % 2
             pairs = g_tiles[t][:].rearrange("p (h e) -> p h e", e=HEAD)[
                 :, first_head : first_head + heads, NOPE:HEAD
@@ -158,34 +175,34 @@ def tile_mla_pb_kernel(tc, x, wq_w, wq_b, cos, sin, grad_out, out):
         w_scales = {}
 
         def pack_unit(n):
-            w_codes[n] = packed.tile(
+            cr = UNIT_ORDER[n]
+            w_codes[cr] = packed.tile(
                 [P, UNIT_PASSES, CHUNK], U32, name="w_codes%d" % n, align_bytes=64
             )
-            w_scales[n] = packed.tile(
+            w_scales[cr] = packed.tile(
                 [P, UNIT_PASSES, CHUNK], U8, name="w_scales%d" % n, align_bytes=64
             )
             words = w_units[n][:].bitcast(F32)
-            for j in range(UNIT_PASSES):
-                for b in range(CHUNK // BANK_ROWS):
+            for b in range(CHUNK // BANK_ROWS):
+                for j in range(UNIT_PASSES):
                     cols = slice(b * BANK_ROWS, (b + 1) * BANK_ROWS)
                     pack_bank(
                         [
                             words[:, 2 * b + i, j * PASS_WORDS : (j + 1) * PASS_WORDS]
                             for i in range(2)
                         ],
-                        w_codes[n][:, j, cols],
-                        w_scales[n][:, j, cols],
+                        w_codes[cr][:, j, cols],
+                        w_scales[cr][:, j, cols],
                         E4M3_X4,
                     )
 
-        def multiply(acc, half, i, n, j):
-            r = n % CHUNK_UNITS
+        def multiply(acc, half, i, c, r, j):
             nc.tensor.matmul_mx(
                 out=acc[:],
                 lhsT=gq_codes[half, r][:, j, i * P : (i + 1) * P].bitcast(E5M2_X4),
                 lhsT_scale=gq_scales[half, r][:, j, i * P : (i + 1) * P],
-                rhs=w_codes[n][:, j, :].bitcast(E4M3_X4),
-                rhs_scale=w_scales[n][:, j, :],
+                rhs=w_codes[c, r][:, j, :].bitcast(E4M3_X4),
+                rhs_scale=w_scales[c, r][:, j, :],
                 start=(r == 0 and j == 0),
                 stop=(r == CHUNK_UNITS - 1 and j == UNIT_PASSES - 1),
             )
@@ -201,44 +218,42 @@ def tile_mla_pb_kernel(tc, x, wq_w, wq_b, cos, sin, grad_out, out):
                 out=out_rows[t * P : (t + 1) * P, c * CHUNK : (c + 1) * CHUNK], in_=res[:]
             )
 
-        rotate(0, 0, HEADS)
-        rotate(1, 0, HEADS)
+        rotate(0, 0)
+        rotate(1, 0)
         pack_unit(0)
         pack_tokens(0, 0)
 
-        pieces = [
-            (t, h) for t in range(HALF_TILES, 2 * HALF_TILES) for h in range(0, HEADS, ROPE_HEADS)
-        ]
-        accs = []
+        late_pieces = [(t, r) for r in range(CHUNK_UNITS) for t in (2, 3)]
+        accs = {}
         for n in range(UNITS):
-            c, r = divmod(n, CHUNK_UNITS)
+            c, r = UNIT_ORDER[n]
             if n + RAW_UNITS < UNITS:
                 load_unit(n + RAW_UNITS)
+            if n in (0, 2):
+                rotate(0, n // 2 + 1)
+                rotate(1, n // 2 + 1)
             if n + 1 < UNITS:
                 pack_unit(n + 1)
-            if n + 1 < CHUNK_UNITS:
-                pack_tokens(0, n + 1)
+            if n in (1, 3):
+                pack_tokens(0, (n + 1) // 2)
             if n >= UNITS - CHUNK_UNITS:
                 pack_tokens(1, n - (UNITS - CHUNK_UNITS))
             if r == 0:
-                accs = [
-                    sums.tile([P, CHUNK], F32, name="acc%d" % i, tag="acc")
-                    for i in range(HALF_TILES)
-                ]
+                for i in range(HALF_TILES):
+                    accs[c, i] = sums.tile([P, CHUNK], F32, name="acc%d" % i, tag="acc")
             for j in range(UNIT_PASSES):
                 for i in range(HALF_TILES):
-                    multiply(accs[i], 0, i, n, j)
-            if 1 <= n <= len(pieces):
-                t, h = pieces[n - 1]
-                rotate(t, h, ROPE_HEADS)
+                    multiply(accs[c, i], 0, i, c, r, j)
+            if 3 <= n < 3 + len(late_pieces):
+                rotate(*late_pieces[n - 3])
             if r == CHUNK_UNITS - 1:
                 for i in range(HALF_TILES):
-                    store(accs[i], 0, i, c)
+                    store(accs[c, i], 0, i, c)
 
         for c in range(CHUNKS):
             for i in range(HALF_TILES):
                 acc = sums.tile([P, CHUNK], F32, tag="acc")
-                for n in range(c * CHUNK_UNITS, (c + 1) * CHUNK_UNITS):
+                for r in range(CHUNK_UNITS):
                     for j in range(UNIT_PASSES):
-                        multiply(acc, 1, i, n, j)
+                        multiply(acc, 1, i, c, r, j)
                 store(acc, 1, i, c)

@@ -38,6 +38,17 @@ ROPE_HEADS_OF = [
     [h for h in range(HEADS) if (h * HEAD + NOPE) // UNIT_K == r] for r in range(CHUNK_UNITS)
 ]
 
+STAGE_BUFS = 4
+UNIT_ORDER = [(c, r) for r in range(CHUNK_UNITS) for c in (0, 1)] + [(c, r) for c in (2, 3) for r in range(CHUNK_UNITS)]
+LOADS_FIRST = [("g",0,0),("g",1,0),("w",0,2),("g",0,1),("g",1,1),("w",1,2),("w",2,1),("g",0,2),("g",1,2),("w",3,1),("g",2,0),("w",4,1),("g",2,1),("g",2,2),("w",5,1),("w",6,1),("g",3,0),("g",3,1),("g",3,2),("w",7,1)]
+LOADS_ROUND = {n: [("w", n + RAW_UNITS, 1)] for n in range(UNITS - RAW_UNITS)}
+ROT_ROUND = {0: [(0,1),(1,1)], 1: [(0,2)], 2: [(1,2)], 3: [(2,0)], 4: [(2,1)], 5: [(2,2)], 6: [(3,0)], 7: [(3,1)], 8: [(3,2)]}
+TOK_ROUND = {1: [(0,1),(1,1)], 3: [(0,2),(1,2)], 4: [(2,0)], 5: [(2,1)], 6: [(2,2)], 7: [(3,0)], 8: [(3,1)], 9: [(3,2)]}
+GROUPS_ROUND = {7: [(0,2,"S")], 8: [(1,2,"S")], 9: [(2,2,"S")], 10: [(0,3,"V"),(1,3,"S")], 11: [(2,3,"V"),(3,2,"S"),(3,3,"V")]}
+W_ENGINES = {}
+ACC_TAG = {0: "accA", 1: "accB", 2: "accA", 3: "accA"}
+STORE_ENGINE = {0: "V", 1: "S"}
+
 FLOPS = 2 * TOKENS * DIM * K
 BYTES = 2 * DIM * K + 2 * TOKENS * K + 4 * TOKENS * DIM + 2 * 2 * 256 * PAIRS
 
@@ -52,11 +63,11 @@ def tile_mla_pb_kernel(tc, x, wq_w, wq_b, cos, sin, grad_out, out):
         const = ctx.enter_context(tc.tile_pool(name="const", bufs=1))
         raw = ctx.enter_context(tc.tile_pool(name="raw", bufs=RAW_UNITS))
         packed = ctx.enter_context(tc.tile_pool(name="packed", bufs=1))
-        stage = ctx.enter_context(tc.tile_pool(name="stage", bufs=8))
+        stage = ctx.enter_context(tc.tile_pool(name="stage", bufs=STAGE_BUFS))
         products = ctx.enter_context(tc.tile_pool(name="products", bufs=2))
         results = ctx.enter_context(tc.tile_pool(name="results", bufs=8))
         turned = ctx.enter_context(tc.psum_pool(name="turned", bufs=4))
-        sums = ctx.enter_context(tc.psum_pool(name="sums", bufs=4))
+        sums = ctx.enter_context(tc.psum_pool(name="sums", bufs=2))
 
         ident = const.tile([P, P], F32)
         make_identity(nc, ident[:])
@@ -77,33 +88,20 @@ def tile_mla_pb_kernel(tc, x, wq_w, wq_b, cos, sin, grad_out, out):
         def load_unit(n, pieces=1):
             c, r = UNIT_ORDER[n]
             w_units[n] = raw.tile([P, CHUNK_TILES, UNIT_K], BF16, name="w_unit", tag="w_unit")
-            step = CHUNK_TILES // pieces
-            for i in range(0, CHUNK_TILES, step):
+            step = UNIT_K // pieces
+            for k0 in range(0, UNIT_K, step):
                 nc.sync.dma_start(
-                    out=w_units[n][:, i : i + step, :],
+                    out=w_units[n][:, :, k0 : k0 + step],
                     in_=wq_w[
-                        c * CHUNK + i * P : c * CHUNK + (i + step) * P, r * UNIT_K : (r + 1) * UNIT_K
+                        c * CHUNK : (c + 1) * CHUNK, r * UNIT_K + k0 : r * UNIT_K + k0 + step
                     ].rearrange("(i p) k -> p i k", p=P),
                 )
 
-        load_tokens(0, 0)
-        load_tokens(1, 0)
-        load_unit(0, 2)
-        load_tokens(0, 1)
-        load_tokens(1, 1)
-        load_unit(1, 2)
-        load_unit(2)
-        load_tokens(0, 2)
-        load_tokens(1, 2)
-        load_unit(3)
-        load_unit(4)
-        for r in range(CHUNK_UNITS):
-            load_tokens(2, r)
-        load_unit(5)
-        for r in range(CHUNK_UNITS):
-            load_tokens(3, r)
-        load_unit(6)
-        load_unit(7)
+        def do_load(item):
+            if item[0] == "g":
+                load_tokens(item[1], item[2])
+            else:
+                load_unit(item[1], item[2])
 
         def rotate(t, r):
             first_head, heads = ROPE_HEADS_OF[r][0], len(ROPE_HEADS_OF[r])
@@ -135,46 +133,44 @@ def tile_mla_pb_kernel(tc, x, wq_w, wq_b, cos, sin, grad_out, out):
                 out=pairs, in0=by_cos[:], in1=by_sin[:].rearrange("p e h j -> p h j e"), op=ADD
             )
 
-        def pack_bank(row_words, codes, scales, fp8_x4):
-            bank = turned.tile([P, 2, BANK_ROWS], F32, tag="bank")
-            for i, words in enumerate(row_words):
-                for u in range(2):
-                    nc.tensor.transpose(
-                        bank[:, u, i * P : (i + 1) * P], words[:, u * P : (u + 1) * P], ident[:]
-                    )
-            grouped = stage.tile([P, 4 * BANK_ROWS], BF16, tag="grouped", align_bytes=64)
-            nc.scalar.copy(
-                out=grouped[:].bitcast(F32).rearrange("p (r u) -> p r u", u=2),
-                in_=bank[:].rearrange("p u r -> p r u"),
-            )
-            nc.vector.quantize_mx(out=codes.bitcast(fp8_x4), scales=scales, in_=grouped[:])
+        def empty(engine, out, in_):
+            if engine == "V":
+                nc.vector.tensor_copy(out=out, in_=in_)
+            else:
+                nc.scalar.copy(out=out, in_=in_)
 
         gq_codes = {}
         gq_scales = {}
 
-        def pack_tokens(half, r):
-            gq_codes[half, r] = packed.tile(
-                [P, UNIT_PASSES, BANK_ROWS], U32, name="gq_codes%d%d" % (half, r), align_bytes=64
+        def pack_tokens(t, r, engine="S"):
+            gq_codes[t, r] = packed.tile(
+                [P, UNIT_PASSES, P], U32, name="gq_codes%d%d" % (t, r), align_bytes=64
             )
-            gq_scales[half, r] = packed.tile(
-                [P, UNIT_PASSES, BANK_ROWS], U8, name="gq_scales%d%d" % (half, r), align_bytes=64
+            gq_scales[t, r] = packed.tile(
+                [P, UNIT_PASSES, P], U8, name="gq_scales%d%d" % (t, r), align_bytes=64
             )
+            words = g_tiles[t][:].bitcast(F32)
+            bank = turned.tile([P, UNIT_PASSES, 2, P], F32, tag="bank")
             for j in range(UNIT_PASSES):
-                first = (r * UNIT_PASSES + j) * PASS_WORDS
-                pack_bank(
-                    [
-                        g_tiles[half * HALF_TILES + i][:].bitcast(F32)[:, first : first + PASS_WORDS]
-                        for i in range(HALF_TILES)
-                    ],
-                    gq_codes[half, r][:, j, :],
-                    gq_scales[half, r][:, j, :],
-                    E5M2_X4,
-                )
+                for u in range(2):
+                    first = (r * UNIT_PASSES + j) * PASS_WORDS + u * P
+                    nc.tensor.transpose(bank[:, j, u, :], words[:, first : first + P], ident[:])
+            grouped = stage.tile([P, UNIT_PASSES * 4 * P], BF16, tag="grouped_g", align_bytes=64)
+            empty(
+                engine,
+                grouped[:].bitcast(F32).rearrange("p (j r u) -> p j r u", j=UNIT_PASSES, u=2),
+                bank[:].rearrange("p j u r -> p j r u"),
+            )
+            nc.vector.quantize_mx(
+                out=gq_codes[t, r][:].rearrange("p j r -> p (j r)").bitcast(E5M2_X4),
+                scales=gq_scales[t, r][:].rearrange("p j r -> p (j r)"),
+                in_=grouped[:],
+            )
 
         w_codes = {}
         w_scales = {}
 
-        def pack_unit(n):
+        def pack_unit(n, engines="SSSS"):
             cr = UNIT_ORDER[n]
             w_codes[cr] = packed.tile(
                 [P, UNIT_PASSES, CHUNK], U32, name="w_codes%d" % n, align_bytes=64
@@ -183,77 +179,89 @@ def tile_mla_pb_kernel(tc, x, wq_w, wq_b, cos, sin, grad_out, out):
                 [P, UNIT_PASSES, CHUNK], U8, name="w_scales%d" % n, align_bytes=64
             )
             words = w_units[n][:].bitcast(F32)
-            for b in range(CHUNK // BANK_ROWS):
-                for j in range(UNIT_PASSES):
-                    cols = slice(b * BANK_ROWS, (b + 1) * BANK_ROWS)
-                    pack_bank(
-                        [
-                            words[:, 2 * b + i, j * PASS_WORDS : (j + 1) * PASS_WORDS]
-                            for i in range(2)
-                        ],
-                        w_codes[cr][:, j, cols],
-                        w_scales[cr][:, j, cols],
-                        E4M3_X4,
+            for j in range(UNIT_PASSES):
+                grouped = stage.tile([P, 4 * CHUNK], BF16, tag="grouped_w", align_bytes=64)
+                for b in range(CHUNK // BANK_ROWS):
+                    bank = turned.tile([P, 2, BANK_ROWS], F32, tag="bank")
+                    for i in range(2):
+                        for u in range(2):
+                            first = j * PASS_WORDS + u * P
+                            nc.tensor.transpose(
+                                bank[:, u, i * P : (i + 1) * P],
+                                words[:, 2 * b + i, first : first + P],
+                                ident[:],
+                            )
+                    empty(
+                        engines[2 * j + b],
+                        grouped[:, b * 4 * BANK_ROWS : (b + 1) * 4 * BANK_ROWS]
+                        .bitcast(F32)
+                        .rearrange("p (r u) -> p r u", u=2),
+                        bank[:].rearrange("p u r -> p r u"),
                     )
+                nc.vector.quantize_mx(
+                    out=w_codes[cr][:, j, :].bitcast(E4M3_X4),
+                    scales=w_scales[cr][:, j, :],
+                    in_=grouped[:],
+                )
 
-        def multiply(acc, half, i, c, r, j):
+        def multiply(acc, t, c, r, j):
             nc.tensor.matmul_mx(
                 out=acc[:],
-                lhsT=gq_codes[half, r][:, j, i * P : (i + 1) * P].bitcast(E5M2_X4),
-                lhsT_scale=gq_scales[half, r][:, j, i * P : (i + 1) * P],
+                lhsT=gq_codes[t, r][:, j, :].bitcast(E5M2_X4),
+                lhsT_scale=gq_scales[t, r][:, j, :],
                 rhs=w_codes[c, r][:, j, :].bitcast(E4M3_X4),
                 rhs_scale=w_scales[c, r][:, j, :],
                 start=(r == 0 and j == 0),
                 stop=(r == CHUNK_UNITS - 1 and j == UNIT_PASSES - 1),
             )
 
-        def store(acc, half, i, c):
-            t = half * HALF_TILES + i
+        def store(acc, t, c, engine):
             res = results.tile([P, CHUNK], F32, tag="res")
-            if i % 2 == 0:
-                nc.vector.tensor_copy(out=res[:], in_=acc[:])
-            else:
-                nc.scalar.copy(out=res[:], in_=acc[:])
+            empty(engine, res[:], acc[:])
             nc.sync.dma_start(
                 out=out_rows[t * P : (t + 1) * P, c * CHUNK : (c + 1) * CHUNK], in_=res[:]
             )
 
+        def group(c, t, engine):
+            acc = sums.tile([P, CHUNK], F32, name="grp", tag="accB")
+            for r in range(CHUNK_UNITS):
+                for j in range(UNIT_PASSES):
+                    multiply(acc, t, c, r, j)
+            store(acc, t, c, engine)
+
+        for item in LOADS_FIRST:
+            do_load(item)
         rotate(0, 0)
         rotate(1, 0)
         pack_unit(0)
         pack_tokens(0, 0)
-
-        late_pieces = [(t, r) for r in range(CHUNK_UNITS) for t in (2, 3)]
+        pack_tokens(1, 0)
         accs = {}
         for n in range(UNITS):
             c, r = UNIT_ORDER[n]
-            if n + RAW_UNITS < UNITS:
-                load_unit(n + RAW_UNITS)
-            if n in (0, 2):
-                rotate(0, n // 2 + 1)
-                rotate(1, n // 2 + 1)
+            for item in LOADS_ROUND.get(n, []):
+                do_load(item)
+            for piece in ROT_ROUND.get(n, []):
+                rotate(*piece)
             if n + 1 < UNITS:
-                pack_unit(n + 1)
-            if n in (1, 3):
-                pack_tokens(0, (n + 1) // 2)
-            if n >= UNITS - CHUNK_UNITS:
-                pack_tokens(1, n - (UNITS - CHUNK_UNITS))
+                pack_unit(n + 1, W_ENGINES.get(n + 1, "SSSS"))
+            for piece in TOK_ROUND.get(n, []):
+                pack_tokens(*piece)
             if r == 0:
-                for i in range(HALF_TILES):
-                    accs[c, i] = sums.tile([P, CHUNK], F32, name="acc%d" % i, tag="acc")
+                for t in (0, 1):
+                    accs[c, t] = sums.tile(
+                        [P, CHUNK], F32, name="acc%d" % t, tag=ACC_TAG[c]
+                    )
             for j in range(UNIT_PASSES):
-                for i in range(HALF_TILES):
-                    multiply(accs[c, i], 0, i, c, r, j)
-            if 3 <= n < 3 + len(late_pieces):
-                rotate(*late_pieces[n - 3])
+                for t in (0, 1):
+                    multiply(accs[c, t], t, c, r, j)
             if r == CHUNK_UNITS - 1:
-                for i in range(HALF_TILES):
-                    store(accs[c, i], 0, i, c)
-
-        for c in range(CHUNKS):
-            for i in range(HALF_TILES):
-                acc = sums.tile([P, CHUNK], F32, tag="acc")
-                for r in range(CHUNK_UNITS):
-                    for j in range(UNIT_PASSES):
-                        multiply(acc, 1, i, c, r, j)
-                store(acc, 1, i, c)
+                for t in (0, 1):
+                    store(accs[c, t], t, c, STORE_ENGINE[t])
+            for g in GROUPS_ROUND.get(n, []):
+                if g[0] == "tok":
+                    pack_tokens(g[1], g[2])
+                elif g[0] == "rot":
+                    rotate(g[1], g[2])
+                else:
+                    group(*g)

@@ -170,16 +170,17 @@ def tile_mla_pb_kernel(tc, x, wq_w, wq_b, cos, sin, grad_out, out):
         w_codes = {}
         w_scales = {}
 
-        def pack_unit(n, engines="SSSS"):
+        def pack_unit(n, passes, engines="SSSS"):
             cr = UNIT_ORDER[n]
-            w_codes[cr] = packed.tile(
-                [P, UNIT_PASSES, CHUNK], U32, name="w_codes%d" % n, align_bytes=64
-            )
-            w_scales[cr] = packed.tile(
-                [P, UNIT_PASSES, CHUNK], U8, name="w_scales%d" % n, align_bytes=64
-            )
+            if cr not in w_codes:
+                w_codes[cr] = packed.tile(
+                    [P, UNIT_PASSES, CHUNK], U32, name="w_codes%d" % n, align_bytes=64
+                )
+                w_scales[cr] = packed.tile(
+                    [P, UNIT_PASSES, CHUNK], U8, name="w_scales%d" % n, align_bytes=64
+                )
             words = w_units[n][:].bitcast(F32)
-            for j in range(UNIT_PASSES):
+            for j in passes:
                 grouped = stage.tile([P, 4 * CHUNK], BF16, tag="grouped_w", align_bytes=64)
                 for b in range(CHUNK // BANK_ROWS):
                     bank = turned.tile([P, 2, BANK_ROWS], F32, tag="bank")
@@ -222,18 +223,23 @@ def tile_mla_pb_kernel(tc, x, wq_w, wq_b, cos, sin, grad_out, out):
                 out=out_rows[t * P : (t + 1) * P, c * CHUNK : (c + 1) * CHUNK], in_=res[:]
             )
 
-        def group(c, t, engine):
-            acc = sums.tile([P, CHUNK], F32, name="grp", tag="accB")
-            for r in range(CHUNK_UNITS):
-                for j in range(UNIT_PASSES):
-                    multiply(acc, t, c, r, j)
-            store(acc, t, c, engine)
+        open_groups = {}
+
+        def group(c, t, engine, part=None):
+            if part != 1:
+                open_groups[c, t] = sums.tile([P, CHUNK], F32, name="grp", tag="accB")
+            acc = open_groups[c, t]
+            for g in range(PASSES):
+                if part is None or g // (PASSES // 2) == part:
+                    multiply(acc, t, c, g // UNIT_PASSES, g % UNIT_PASSES)
+            if part != 0:
+                store(acc, t, c, engine)
 
         for item in LOADS_FIRST:
             do_load(item)
         rotate(0, 0)
         rotate(1, 0)
-        pack_unit(0)
+        pack_unit(0, (0, 1))
         pack_tokens(0, 0)
         pack_tokens(1, 0)
         accs = {}
@@ -243,25 +249,25 @@ def tile_mla_pb_kernel(tc, x, wq_w, wq_b, cos, sin, grad_out, out):
                 do_load(item)
             for piece in ROT_ROUND.get(n, []):
                 rotate(*piece)
-            if n + 1 < UNITS:
-                pack_unit(n + 1, W_ENGINES.get(n + 1, "SSSS"))
-            for piece in TOK_ROUND.get(n, []):
-                pack_tokens(*piece)
             if r == 0:
                 for t in (0, 1):
                     accs[c, t] = sums.tile(
                         [P, CHUNK], F32, name="acc%d" % t, tag=ACC_TAG[c]
                     )
+            groups = GROUPS_ROUND.get(n, [])
             for j in range(UNIT_PASSES):
+                if n + 1 < UNITS:
+                    pack_unit(n + 1, (j,))
+                if j == 0:
+                    for piece in TOK_ROUND.get(n, []):
+                        pack_tokens(*piece)
                 for t in (0, 1):
                     multiply(accs[c, t], t, c, r, j)
+                if n + 1 < UNITS and len(groups) == 1:
+                    group(*groups[0], part=j)
             if r == CHUNK_UNITS - 1:
                 for t in (0, 1):
                     store(accs[c, t], t, c, STORE_ENGINE[t])
-            for g in GROUPS_ROUND.get(n, []):
-                if g[0] == "tok":
-                    pack_tokens(g[1], g[2])
-                elif g[0] == "rot":
-                    rotate(g[1], g[2])
-                else:
+            if n + 1 == UNITS or len(groups) > 1:
+                for g in groups:
                     group(*g)

@@ -48,6 +48,8 @@ GROUPS_ROUND = {7: [(0,2,"S")], 8: [(1,2,"S")], 9: [(2,2,"S")], 10: [(0,3,"V"),(
 W_ENGINES = {}
 ACC_TAG = {0: "accA", 1: "accB", 2: "accA", 3: "accA"}
 STORE_ENGINE = {0: "V", 1: "S"}
+AWAKE_FIRST = 6
+AWAKE_BETWEEN = 2
 
 FLOPS = 2 * TOKENS * DIM * K
 BYTES = 2 * DIM * K + 2 * TOKENS * K + 4 * TOKENS * DIM + 2 * 2 * 256 * PAIRS
@@ -237,11 +239,26 @@ def tile_mla_pb_kernel(tc, x, wq_w, wq_b, cos, sin, grad_out, out):
 
         for item in LOADS_FIRST:
             do_load(item)
+        zeros = const.tile([P, CHUNK], BF16, name="zeros")
+        nc.gpsimd.memset(zeros[:], 0.0)
+        idle_sum = sums.tile([P, CHUNK], F32, name="idle_sum", tag="accB")
+
+        def keep_awake(count):
+            for i in range(count):
+                nc.tensor.matmul(
+                    out=idle_sum[:], lhsT=zeros[:, 0:P], rhs=zeros[:], start=True, stop=True
+                )
+
         rotate(0, 0)
         rotate(1, 0)
-        pack_unit(0, (0, 1))
+        keep_awake(AWAKE_FIRST)
+        pack_unit(0, (0,))
+        keep_awake(AWAKE_BETWEEN)
+        pack_unit(0, (1,))
+        keep_awake(AWAKE_BETWEEN)
         pack_tokens(0, 0)
         pack_tokens(1, 0)
+        keep_awake(AWAKE_BETWEEN)
         accs = {}
         for n in range(UNITS):
             c, r = UNIT_ORDER[n]

@@ -40,7 +40,7 @@ ROPE_HEADS_OF = [
 
 STAGE_BUFS = 4
 UNIT_ORDER = [(c, r) for r in range(CHUNK_UNITS) for c in (0, 1)] + [(c, r) for c in (2, 3) for r in range(CHUNK_UNITS)]
-LOADS_FIRST = [("g",0,0),("g",1,0),("w",0,2),("g",0,1),("g",1,1),("w",1,2),("w",2,1),("g",0,2),("g",1,2),("w",3,1),("g",2,0),("w",4,1),("g",2,1),("g",2,2),("w",5,1),("w",6,1),("g",3,0),("g",3,1),("g",3,2),("w",7,1)]
+LOADS_FIRST = [("g",0,0),("w",0,2,0),("g",1,0),("w",0,2,1),("g",0,1),("g",1,1),("w",1,2),("w",2,1),("g",0,2),("g",1,2),("w",3,1),("g",2,0),("w",4,1),("g",2,1),("g",2,2),("w",5,1),("w",6,1),("g",3,0),("g",3,1),("g",3,2),("w",7,1)]
 LOADS_ROUND = {n: [("w", n + RAW_UNITS, 1)] for n in range(UNITS - RAW_UNITS)}
 ROT_ROUND = {0: [(0,1),(1,1)], 1: [(0,2)], 2: [(1,2)], 3: [(2,0)], 4: [(2,1)], 5: [(2,2)], 6: [(3,0)], 7: [(3,1)], 8: [(3,2)]}
 TOK_ROUND = {1: [(0,1),(1,1)], 3: [(0,2),(1,2)], 4: [(2,0)], 5: [(2,1)], 6: [(2,2)], 7: [(3,0)], 8: [(3,1)], 9: [(3,2)]}
@@ -50,6 +50,7 @@ ACC_TAG = {0: "accA", 1: "accB", 2: "accA", 3: "accA"}
 STORE_ENGINE = {0: "V", 1: "S"}
 AWAKE_FIRST = 6
 AWAKE_BETWEEN = 2
+LAST_PIECES = 2
 
 FLOPS = 2 * TOKENS * DIM * K
 BYTES = 2 * DIM * K + 2 * TOKENS * K + 4 * TOKENS * DIM + 2 * 2 * 256 * PAIRS
@@ -87,11 +88,12 @@ def tile_mla_pb_kernel(tc, x, wq_w, wq_b, cos, sin, grad_out, out):
             cols = slice(r * UNIT_K, (r + 1) * UNIT_K)
             nc.sync.dma_start(out=g_tiles[t][:, cols], in_=g_rows[t * P : (t + 1) * P, cols])
 
-        def load_unit(n, pieces=1):
+        def load_unit(n, pieces=1, only=None):
             c, r = UNIT_ORDER[n]
-            w_units[n] = raw.tile([P, CHUNK_TILES, UNIT_K], BF16, name="w_unit", tag="w_unit")
+            if n not in w_units:
+                w_units[n] = raw.tile([P, CHUNK_TILES, UNIT_K], BF16, name="w_unit", tag="w_unit")
             step = UNIT_K // pieces
-            for k0 in range(0, UNIT_K, step):
+            for k0 in range(0, UNIT_K, step) if only is None else (only * step,):
                 nc.sync.dma_start(
                     out=w_units[n][:, :, k0 : k0 + step],
                     in_=wq_w[
@@ -103,7 +105,7 @@ def tile_mla_pb_kernel(tc, x, wq_w, wq_b, cos, sin, grad_out, out):
             if item[0] == "g":
                 load_tokens(item[1], item[2])
             else:
-                load_unit(item[1], item[2])
+                load_unit(*item[1:])
 
         def rotate(t, r):
             first_head, heads = ROPE_HEADS_OF[r][0], len(ROPE_HEADS_OF[r])
@@ -220,10 +222,14 @@ def tile_mla_pb_kernel(tc, x, wq_w, wq_b, cos, sin, grad_out, out):
 
         def store(acc, t, c, engine):
             res = results.tile([P, CHUNK], F32, tag="res")
-            empty(engine, res[:], acc[:])
-            nc.sync.dma_start(
-                out=out_rows[t * P : (t + 1) * P, c * CHUNK : (c + 1) * CHUNK], in_=res[:]
-            )
+            pieces = LAST_PIECES if (c, t) == (CHUNKS - 1, TOKENS // P - 1) else 1
+            step = CHUNK // pieces
+            for d0 in range(0, CHUNK, step):
+                empty(engine, res[:, d0 : d0 + step], acc[:, d0 : d0 + step])
+                nc.sync.dma_start(
+                    out=out_rows[t * P : (t + 1) * P, c * CHUNK + d0 : c * CHUNK + d0 + step],
+                    in_=res[:, d0 : d0 + step],
+                )
 
         open_groups = {}
 

@@ -72,7 +72,7 @@ def tile_mla_pb_kernel(tc, x, wq_w, wq_b, cos, sin, grad_out, out):
         turned = ctx.enter_context(tc.psum_pool(name="turned", bufs=4))
         sums = ctx.enter_context(tc.psum_pool(name="sums", bufs=2))
 
-        ident = const.tile([P, P], F32)
+        ident = const.tile([P, P], F32, align_bytes=256)
         make_identity(nc, ident[:])
         cos_sb = const.tile([P, 2, PAIRS], BF16)
         sin_sb = const.tile([P, 2, PAIRS], BF16)
@@ -81,7 +81,7 @@ def tile_mla_pb_kernel(tc, x, wq_w, wq_b, cos, sin, grad_out, out):
         neg_sin = const.tile([P, 2, PAIRS], BF16)
         nc.vector.tensor_scalar_mul(out=neg_sin[:], in0=sin_sb[:], scalar1=-1.0)
 
-        g_tiles = [const.tile([P, K], BF16, name="g%d" % t) for t in range(TOKENS // P)]
+        g_tiles = [const.tile([P, K], BF16, name="g%d" % t, align_bytes=256) for t in range(TOKENS // P)]
         w_units = {}
 
         def load_tokens(t, r):
@@ -91,7 +91,7 @@ def tile_mla_pb_kernel(tc, x, wq_w, wq_b, cos, sin, grad_out, out):
         def load_unit(n, pieces=1, only=None):
             c, r = UNIT_ORDER[n]
             if n not in w_units:
-                w_units[n] = raw.tile([P, CHUNK_TILES, UNIT_K], BF16, name="w_unit", tag="w_unit")
+                w_units[n] = raw.tile([P, CHUNK_TILES, UNIT_K], BF16, name="w_unit", tag="w_unit", align_bytes=256)
             step = UNIT_K // pieces
             for k0 in range(0, UNIT_K, step) if only is None else (only * step,):
                 nc.sync.dma_start(
@@ -148,10 +148,10 @@ def tile_mla_pb_kernel(tc, x, wq_w, wq_b, cos, sin, grad_out, out):
 
         def pack_tokens(t, r, engine="S"):
             gq_codes[t, r] = packed.tile(
-                [P, UNIT_PASSES, P], U32, name="gq_codes%d%d" % (t, r), align_bytes=64
+                [P, UNIT_PASSES, P], U32, name="gq_codes%d%d" % (t, r), align_bytes=256
             )
             gq_scales[t, r] = packed.tile(
-                [P, UNIT_PASSES, P], U8, name="gq_scales%d%d" % (t, r), align_bytes=64
+                [P, UNIT_PASSES, P], U8, name="gq_scales%d%d" % (t, r), align_bytes=256
             )
             words = g_tiles[t][:].bitcast(F32)
             bank = turned.tile([P, UNIT_PASSES, 2, P], F32, tag="bank")
@@ -159,7 +159,7 @@ def tile_mla_pb_kernel(tc, x, wq_w, wq_b, cos, sin, grad_out, out):
                 for u in range(2):
                     first = (r * UNIT_PASSES + j) * PASS_WORDS + u * P
                     nc.tensor.transpose(bank[:, j, u, :], words[:, first : first + P], ident[:])
-            grouped = stage.tile([P, UNIT_PASSES * 4 * P], BF16, tag="grouped_g", align_bytes=64)
+            grouped = stage.tile([P, UNIT_PASSES * 4 * P], BF16, tag="grouped_g", align_bytes=256)
             empty(
                 engine,
                 grouped[:].bitcast(F32).rearrange("p (j r u) -> p j r u", j=UNIT_PASSES, u=2),
@@ -178,14 +178,14 @@ def tile_mla_pb_kernel(tc, x, wq_w, wq_b, cos, sin, grad_out, out):
             cr = UNIT_ORDER[n]
             if cr not in w_codes:
                 w_codes[cr] = packed.tile(
-                    [P, UNIT_PASSES, CHUNK], U32, name="w_codes%d" % n, align_bytes=64
+                    [P, UNIT_PASSES, CHUNK], U32, name="w_codes%d" % n, align_bytes=256
                 )
                 w_scales[cr] = packed.tile(
-                    [P, UNIT_PASSES, CHUNK], U8, name="w_scales%d" % n, align_bytes=64
+                    [P, UNIT_PASSES, CHUNK], U8, name="w_scales%d" % n, align_bytes=256
                 )
             words = w_units[n][:].bitcast(F32)
             for j in passes:
-                grouped = stage.tile([P, 4 * CHUNK], BF16, tag="grouped_w", align_bytes=64)
+                grouped = stage.tile([P, 4 * CHUNK], BF16, tag="grouped_w", align_bytes=256)
                 for b in range(CHUNK // BANK_ROWS):
                     bank = turned.tile([P, 2, BANK_ROWS], F32, tag="bank")
                     for i in range(2):

@@ -43,7 +43,7 @@ UNIT_ORDER = [(c, r) for r in range(CHUNK_UNITS) for c in (0, 1)] + [(c, r) for 
 LOADS_FIRST = [("g",0,0),("w",0,2,0),("g",1,0),("w",0,2,1),("g",0,1),("g",1,1),("w",1,2),("w",2,1),("g",0,2),("g",1,2),("w",3,1),("g",2,0),("w",4,1),("g",2,1),("g",2,2),("w",5,1),("w",6,1),("g",3,0),("g",3,1),("g",3,2),("w",7,1)]
 LOADS_ROUND = {n: [("w", n + RAW_UNITS, 1)] for n in range(UNITS - RAW_UNITS)}
 ROT_ROUND = {0: [(0,1),(1,1)], 1: [(0,2)], 2: [(1,2)], 3: [(2,0)], 4: [(2,1)], 5: [(2,2)], 6: [(3,0)], 7: [(3,1)], 8: [(3,2)]}
-TOK_ROUND = {1: [(0,1),(1,1)], 3: [(0,2),(1,2)], 4: [(2,0)], 5: [(2,1)], 6: [(2,2)], 7: [(3,0)], 8: [(3,1)], 9: [(3,2)]}
+TOK_HALF = {1: [(0,1)], 2: [(1,1)], 5: [(0,2)], 6: [(1,2)], 8: [(2,0)], 10: [(2,1)], 12: [(2,2)], 14: [(3,0)], 16: [(3,1)], 18: [(3,2)]}
 GROUPS_ROUND = {7: [(0,2,"S")], 8: [(1,2,"S")], 9: [(2,2,"S")], 10: [(0,3,"V"),(1,3,"S")], 11: [(2,3,"V"),(3,2,"S"),(3,3,"V")]}
 W_ENGINES = {}
 ACC_TAG = {0: "accA", 1: "accB", 2: "accA", 3: "accA"}
@@ -281,9 +281,8 @@ def tile_mla_pb_kernel(tc, x, wq_w, wq_b, cos, sin, grad_out, out):
             for j in range(UNIT_PASSES):
                 if n + 1 < UNITS:
                     pack_unit(n + 1, (j,))
-                if j == 0:
-                    for piece in TOK_ROUND.get(n, []):
-                        pack_tokens(*piece)
+                for piece in TOK_HALF.get(2 * n + j, []):
+                    pack_tokens(*piece)
                 for t in (0, 1):
                     multiply(accs[c, t], t, c, r, j)
                 if n + 1 < UNITS and len(groups) == 1:

@@ -38,13 +38,19 @@ ROPE_HEADS_OF = [
     [h for h in range(HEADS) if (h * HEAD + NOPE) // UNIT_K == r] for r in range(CHUNK_UNITS)
 ]
 
+TURNED_UNITS = (10, 11)
+TURN_LEAD = 1
+ROW_BLOCKS = CHUNK // 32
 STAGE_BUFS = 4
 UNIT_ORDER = [(c, r) for r in range(CHUNK_UNITS) for c in (0, 1)] + [(c, r) for c in (2, 3) for r in range(CHUNK_UNITS)]
 LOADS_FIRST = [("g",0,0),("w",0,2,0),("g",1,0),("w",0,2,1),("g",0,1),("g",1,1),("w",1,2),("w",2,1),("g",0,2),("g",1,2),("w",3,1),("g",2,0),("w",4,1),("g",2,1),("g",2,2),("w",5,1),("w",6,1),("g",3,0),("g",3,1),("g",3,2),("w",7,1)]
-LOADS_ROUND = {n: [("w", n + RAW_UNITS, 1)] for n in range(UNITS - RAW_UNITS)}
+LOADS_ROUND = {0: [("w", 8, 1)], 1: [("w", 9, 1)], 5: [("w", 10, 1)], 6: [("w", 11, 1)]}
 ROT_ROUND = {0: [(0,1),(1,1)], 1: [(0,2)], 2: [(1,2)], 3: [(2,0)], 4: [(2,1)], 5: [(2,2)], 6: [(3,0)], 7: [(3,1)], 8: [(3,2)]}
 TOK_HALF = {1: [(0,1)], 2: [(1,1)], 5: [(0,2)], 6: [(1,2)], 8: [(2,0)], 10: [(2,1)], 12: [(2,2)], 14: [(3,0)], 16: [(3,1)], 18: [(3,2)]}
-GROUPS_ROUND = {7: [(0,2,"S")], 8: [(1,2,"S")], 9: [(2,2,"S")], 10: [(0,3,"V"),(1,3,"S")], 11: [(2,3,"V"),(3,2,"S"),(3,3,"V")]}
+LATE = [(0, 2), (1, 2), (2, 2), (0, 3), (1, 3), (2, 3), (3, 2), (3, 3)]
+LATE_ENGINE = {(0, 3): "V", (2, 3): "V", (3, 3): "V"}
+LATE_BEFORE = {16: 3, 17: 3, 18: 3, 19: 3, 20: 6, 21: 6, 22: 6}
+LATE_AFTER = {14: 3, 15: 3}
 W_ENGINES = {}
 ACC_TAG = {0: "accA", 1: "accB", 2: "accA", 3: "accA"}
 STORE_ENGINE = {0: "V", 1: "S"}
@@ -67,6 +73,7 @@ def tile_mla_pb_kernel(tc, x, wq_w, wq_b, cos, sin, grad_out, out):
         raw = ctx.enter_context(tc.tile_pool(name="raw", bufs=RAW_UNITS))
         packed = ctx.enter_context(tc.tile_pool(name="packed", bufs=1))
         stage = ctx.enter_context(tc.tile_pool(name="stage", bufs=STAGE_BUFS))
+        blocks = ctx.enter_context(tc.tile_pool(name="blocks", bufs=2))
         products = ctx.enter_context(tc.tile_pool(name="products", bufs=2))
         results = ctx.enter_context(tc.tile_pool(name="results", bufs=8))
         turned = ctx.enter_context(tc.psum_pool(name="turned", bufs=4))
@@ -90,6 +97,20 @@ def tile_mla_pb_kernel(tc, x, wq_w, wq_b, cos, sin, grad_out, out):
 
         def load_unit(n, pieces=1, only=None):
             c, r = UNIT_ORDER[n]
+            if n in TURNED_UNITS:
+                w_units[n] = raw.tile(
+                    [P, UNIT_PASSES * 2, ROW_BLOCKS, 64], BF16, name="w_unit", tag="w_unit", align_bytes=256
+                )
+                for m in range(UNIT_PASSES * 2):
+                    for q in range(4):
+                        k0 = r * UNIT_K + m * 256 + q * 64
+                        nc.sync.dma_start(
+                            out=w_units[n][32 * q : 32 * q + 32, m, :, :],
+                            in_=wq_w[c * CHUNK : (c + 1) * CHUNK, k0 : k0 + 64].rearrange(
+                                "(i b) k -> b i k", b=32
+                            ),
+                        )
+                return
             if n not in w_units:
                 w_units[n] = raw.tile([P, CHUNK_TILES, UNIT_K], BF16, name="w_unit", tag="w_unit", align_bytes=256)
             step = UNIT_K // pieces
@@ -174,6 +195,15 @@ def tile_mla_pb_kernel(tc, x, wq_w, wq_b, cos, sin, grad_out, out):
         w_codes = {}
         w_scales = {}
 
+        turned_units = {}
+
+        def turn_unit(n, j):
+            turned_units[n, j] = blocks.tile([P, 2 * CHUNK], F32, name="turned_pass", align_bytes=256)
+            nc.vector.transpose(
+                out=turned_units[n, j][:],
+                in_=w_units[n][:, 2 * j : 2 * j + 2].rearrange("p u i k -> p (u i k)").bitcast(F32),
+            )
+
         def pack_unit(n, passes, engines="SSSS"):
             cr = UNIT_ORDER[n]
             if cr not in w_codes:
@@ -183,9 +213,20 @@ def tile_mla_pb_kernel(tc, x, wq_w, wq_b, cos, sin, grad_out, out):
                 w_scales[cr] = packed.tile(
                     [P, UNIT_PASSES, CHUNK], U8, name="w_scales%d" % n, align_bytes=256
                 )
-            words = w_units[n][:].bitcast(F32)
             for j in passes:
                 grouped = stage.tile([P, 4 * CHUNK], BF16, tag="grouped_w", align_bytes=256)
+                if n in TURNED_UNITS:
+                    nc.scalar.copy(
+                        out=grouped[:].bitcast(F32).rearrange("p (c u) -> p c u", u=2),
+                        in_=turned_units[n, j][:].rearrange("p (u c) -> p c u", u=2),
+                    )
+                    nc.vector.quantize_mx(
+                        out=w_codes[cr][:, j, :].bitcast(E4M3_X4),
+                        scales=w_scales[cr][:, j, :],
+                        in_=grouped[:],
+                    )
+                    continue
+                words = w_units[n][:].bitcast(F32)
                 for b in range(CHUNK // BANK_ROWS):
                     bank = turned.tile([P, 2, BANK_ROWS], F32, tag="bank")
                     for i in range(2):
@@ -232,16 +273,17 @@ def tile_mla_pb_kernel(tc, x, wq_w, wq_b, cos, sin, grad_out, out):
                 )
 
         open_groups = {}
+        late = [(c, t, g) for c, t in LATE for g in range(PASSES)]
 
-        def group(c, t, engine, part=None):
-            if part != 1:
-                open_groups[c, t] = sums.tile([P, CHUNK], F32, name="grp", tag="accB")
-            acc = open_groups[c, t]
-            for g in range(PASSES):
-                if part is None or g // (PASSES // 2) == part:
-                    multiply(acc, t, c, g // UNIT_PASSES, g % UNIT_PASSES)
-            if part != 0:
-                store(acc, t, c, engine)
+        def multiply_late(number):
+            for c, t, g in late[:number]:
+                if g == 0:
+                    open_groups[c, t] = sums.tile([P, CHUNK], F32, name="grp", tag="accB")
+                multiply(open_groups[c, t], t, c, g // UNIT_PASSES, g % UNIT_PASSES)
+                if g == PASSES - 1:
+                    store(open_groups[c, t], t, c, LATE_ENGINE.get((c, t), "S"))
+            for i in range(min(number, len(late))):
+                late.remove(late[0])
 
         for item in LOADS_FIRST:
             do_load(item)
@@ -277,19 +319,19 @@ def tile_mla_pb_kernel(tc, x, wq_w, wq_b, cos, sin, grad_out, out):
                     accs[c, t] = sums.tile(
                         [P, CHUNK], F32, name="acc%d" % t, tag=ACC_TAG[c]
                     )
-            groups = GROUPS_ROUND.get(n, [])
             for j in range(UNIT_PASSES):
+                q = 2 * (n + 1) + j + TURN_LEAD
+                if q // 2 in TURNED_UNITS:
+                    turn_unit(q // 2, q % 2)
                 if n + 1 < UNITS:
                     pack_unit(n + 1, (j,))
                 for piece in TOK_HALF.get(2 * n + j, []):
                     pack_tokens(*piece)
+                multiply_late(LATE_BEFORE.get(2 * n + j, 0))
                 for t in (0, 1):
                     multiply(accs[c, t], t, c, r, j)
-                if n + 1 < UNITS and len(groups) == 1:
-                    group(*groups[0], part=j)
+                multiply_late(LATE_AFTER.get(2 * n + j, 0))
             if r == CHUNK_UNITS - 1:
                 for t in (0, 1):
                     store(accs[c, t], t, c, STORE_ENGINE[t])
-            if n + 1 == UNITS or len(groups) > 1:
-                for g in groups:
-                    group(*g)
+        multiply_late(len(late))

@@ -44,13 +44,13 @@ ROW_BLOCKS = CHUNK // 32
 STAGE_BUFS = 4
 UNIT_ORDER = [(c, r) for r in range(CHUNK_UNITS) for c in (0, 1)] + [(c, r) for c in (2, 3) for r in range(CHUNK_UNITS)]
 LOADS_FIRST = [("g",0,0),("w",0,2,0),("g",1,0),("w",0,2,1),("g",0,1),("g",1,1),("w",1,2),("w",2,1),("g",0,2),("g",1,2),("w",3,1),("g",2,0),("w",4,1),("g",2,1),("g",2,2),("w",5,1),("w",6,1),("g",3,0),("g",3,1),("g",3,2),("w",7,1)]
-LOADS_ROUND = {0: [("w", 8, 1)], 1: [("w", 9, 1)], 5: [("w", 10, 1)], 6: [("w", 11, 1)]}
+LOADS_ROUND = {0: [("w", 8, 1)], 1: [("w", 9, 1)], 4: [("w", 10, 1)], 5: [("w", 11, 1)]}
 ROT_ROUND = {0: [(0,1),(1,1)], 1: [(0,2)], 2: [(1,2)], 3: [(2,0)], 4: [(2,1)], 5: [(2,2)], 6: [(3,0)], 7: [(3,1)], 8: [(3,2)]}
 TOK_HALF = {1: [(0,1)], 2: [(1,1)], 5: [(0,2)], 6: [(1,2)], 8: [(2,0)], 10: [(2,1)], 12: [(2,2)], 14: [(3,0)], 16: [(3,1)], 18: [(3,2)]}
 LATE = [(0, 2), (1, 2), (2, 2), (0, 3), (1, 3), (2, 3), (3, 2), (3, 3)]
-LATE_ENGINE = {(0, 3): "V", (2, 3): "V", (3, 3): "V"}
-LATE_BEFORE = {16: 3, 17: 3, 18: 3, 19: 3, 20: 6, 21: 6, 22: 6}
-LATE_AFTER = {14: 3, 15: 3}
+LATE_ENGINE = {(3, 3): "V"}
+LATE_BEFORE = {14: 3, 15: 3, 16: 3, 17: 3, 18: 3, 19: 3, 20: 6, 21: 6, 22: 6}
+LATE_AFTER = {}
 W_ENGINES = {}
 ACC_TAG = {0: "accA", 1: "accB", 2: "accA", 3: "accA"}
 STORE_ENGINE = {0: "V", 1: "S"}

from contextlib import ExitStack

import concourse.mybir as mybir
from concourse.masks import make_identity

F32 = mybir.dt.float32
BF16 = mybir.dt.bfloat16
U32 = mybir.dt.uint32
U8 = mybir.dt.uint8
E4M3_X4 = mybir.dt.float8_e4m3fn_x4
E5M2_X4 = mybir.dt.float8_e5m2_x4
MULT = mybir.AluOpType.mult
ADD = mybir.AluOpType.add

P = 128
TOKENS = 512
DIM = 2048
HEADS = 16
HEAD = 192
NOPE = 128
PAIRS = 32
K = HEADS * HEAD

PASS_WORDS = 256
PASSES = K // (2 * PASS_WORDS)
CHUNK = 512
CHUNKS = DIM // CHUNK
CHUNK_TILES = CHUNK // P
UNIT_PASSES = 2
CHUNK_UNITS = PASSES // UNIT_PASSES
UNITS = CHUNKS * CHUNK_UNITS
UNIT_K = UNIT_PASSES * 2 * PASS_WORDS
HALF_TILES = 2
BANK_ROWS = 2 * P
RAW_UNITS = 8
UNIT_ORDER = [(c, r) for pair in (0, 2) for r in range(CHUNK_UNITS) for c in (pair, pair + 1)]
ROPE_HEADS_OF = [
    [h for h in range(HEADS) if (h * HEAD + NOPE) // UNIT_K == r] for r in range(CHUNK_UNITS)
]

TURNED_UNITS = (10, 11)
TURN_LEAD = 1
ROW_BLOCKS = CHUNK // 32
STAGE_BUFS = 4
UNIT_ORDER = [(c, r) for r in range(CHUNK_UNITS) for c in (0, 1)] + [(c, r) for c in (2, 3) for r in range(CHUNK_UNITS)]
LOADS_FIRST = [("g",0,0),("w",0,2,0),("g",1,0),("w",0,2,1),("g",0,1),("g",1,1),("w",1,2),("w",2,1),("g",0,2),("g",1,2),("w",3,1),("g",2,0),("w",4,1),("g",2,1),("g",2,2),("w",5,1),("w",6,1),("g",3,0),("g",3,1),("g",3,2),("w",7,1)]
LOADS_ROUND = {0: [("w", 8, 1)], 1: [("w", 9, 1)], 4: [("w", 10, 1)], 5: [("w", 11, 1)]}
ROT_ROUND = {0: [(0,1),(1,1)], 1: [(0,2)], 2: [(1,2)], 3: [(2,0)], 4: [(2,1)], 5: [(2,2)], 6: [(3,0)], 7: [(3,1)], 8: [(3,2)]}
TOK_HALF = {1: [(0,1)], 2: [(1,1)], 5: [(0,2)], 6: [(1,2)], 8: [(2,0)], 10: [(2,1)], 12: [(2,2)], 14: [(3,0)], 16: [(3,1)], 18: [(3,2)]}
LATE = [(0, 2), (1, 2), (2, 2), (0, 3), (1, 3), (2, 3), (3, 2), (3, 3)]
LATE_ENGINE = {(3, 3): "V"}
LATE_BEFORE = {14: 3, 15: 3, 16: 3, 17: 3, 18: 3, 19: 3, 20: 6, 21: 6, 22: 6}
LATE_AFTER = {}
W_ENGINES = {}
ACC_TAG = {0: "accA", 1: "accB", 2: "accA", 3: "accA"}
STORE_ENGINE = {0: "V", 1: "S"}
AWAKE_FIRST = 6
AWAKE_BETWEEN = 2
LAST_PIECES = 2

FLOPS = 2 * TOKENS * DIM * K
BYTES = 2 * DIM * K + 2 * TOKENS * K + 4 * TOKENS * DIM + 2 * 2 * 256 * PAIRS


def tile_mla_pb_kernel(tc, x, wq_w, wq_b, cos, sin, grad_out, out):
    nc = tc.nc
    g_rows = grad_out.rearrange("b s h e -> (b s) (h e)")
    out_rows = out.rearrange("b s d -> (b s) d")

    with ExitStack() as ctx:
        ctx.enter_context(tc.manual_schedule())
        const = ctx.enter_context(tc.tile_pool(name="const", bufs=1))
        raw = ctx.enter_context(tc.tile_pool(name="raw", bufs=RAW_UNITS))
        packed = ctx.enter_context(tc.tile_pool(name="packed", bufs=1))
        stage = ctx.enter_context(tc.tile_pool(name="stage", bufs=STAGE_BUFS))
        blocks = ctx.enter_context(tc.tile_pool(name="blocks", bufs=2))
        products = ctx.enter_context(tc.tile_pool(name="products", bufs=2))
        results = ctx.enter_context(tc.tile_pool(name="results", bufs=8))
        turned = ctx.enter_context(tc.psum_pool(name="turned", bufs=4))
        sums = ctx.enter_context(tc.psum_pool(name="sums", bufs=2))

        ident = const.tile([P, P], F32, align_bytes=256)
        make_identity(nc, ident[:])
        cos_sb = const.tile([P, 2, PAIRS], BF16)
        sin_sb = const.tile([P, 2, PAIRS], BF16)
        nc.scalar.dma_start(out=cos_sb[:], in_=cos.rearrange("(s p) j -> p s j", p=P))
        nc.scalar.dma_start(out=sin_sb[:], in_=sin.rearrange("(s p) j -> p s j", p=P))
        neg_sin = const.tile([P, 2, PAIRS], BF16)
        nc.vector.tensor_scalar_mul(out=neg_sin[:], in0=sin_sb[:], scalar1=-1.0)

        g_tiles = [const.tile([P, K], BF16, name="g%d" % t, align_bytes=256) for t in range(TOKENS // P)]
        w_units = {}

        def load_tokens(t, r):
            cols = slice(r * UNIT_K, (r + 1) * UNIT_K)
            nc.sync.dma_start(out=g_tiles[t][:, cols], in_=g_rows[t * P : (t + 1) * P, cols])

        def load_unit(n, pieces=1, only=None):
            c, r = UNIT_ORDER[n]
            if n in TURNED_UNITS:
                w_units[n] = raw.tile(
                    [P, UNIT_PASSES * 2, ROW_BLOCKS, 64], BF16, name="w_unit", tag="w_unit", align_bytes=256
                )
                for m in range(UNIT_PASSES * 2):
                    for q in range(4):
                        k0 = r * UNIT_K + m * 256 + q * 64
                        nc.sync.dma_start(
                            out=w_units[n][32 * q : 32 * q + 32, m, :, :],
                            in_=wq_w[c * CHUNK : (c + 1) * CHUNK, k0 : k0 + 64].rearrange(
                                "(i b) k -> b i k", b=32
                            ),
                        )
                return
            if n not in w_units:
                w_units[n] = raw.tile([P, CHUNK_TILES, UNIT_K], BF16, name="w_unit", tag="w_unit", align_bytes=256)
            step = UNIT_K // pieces
            for k0 in range(0, UNIT_K, step) if only is None else (only * step,):
                nc.sync.dma_start(
                    out=w_units[n][:, :, k0 : k0 + step],
                    in_=wq_w[
                        c * CHUNK : (c + 1) * CHUNK, r * UNIT_K + k0 : r * UNIT_K + k0 + step
                    ].rearrange("(i p) k -> p i k", p=P),
                )

        def do_load(item):
            if item[0] == "g":
                load_tokens(item[1], item[2])
            else:
                load_unit(*item[1:])

        def rotate(t, r):
            first_head, heads = ROPE_HEADS_OF[r][0], len(ROPE_HEADS_OF[r])
            s = t % 2
            pairs = g_tiles[t][:].rearrange("p (h e) -> p h e", e=HEAD)[
                :, first_head : first_head + heads, NOPE:HEAD
            ].rearrange("p h (j e) -> p h j e", e=2)
            by_cos = products.tile([P, heads, PAIRS, 2], F32, tag="by_cos")
            by_sin = products.tile([P, 2, heads, PAIRS], F32, tag="by_sin")
            nc.vector.tensor_tensor(
                out=by_cos[:],
                in0=pairs,
                in1=cos_sb[:, s, :].unsqueeze(1).unsqueeze(3).to_broadcast([P, heads, PAIRS, 2]),
                op=MULT,
            )
            nc.vector.tensor_tensor(
                out=by_sin[:, 0],
                in0=pairs[:, :, :, 1],
                in1=sin_sb[:, s, :].unsqueeze(1).to_broadcast([P, heads, PAIRS]),
                op=MULT,
            )
            nc.vector.tensor_tensor(
                out=by_sin[:, 1],
                in0=pairs[:, :, :, 0],
                in1=neg_sin[:, s, :].unsqueeze(1).to_broadcast([P, heads, PAIRS]),
                op=MULT,
            )
            nc.vector.tensor_tensor(
                out=pairs, in0=by_cos[:], in1=by_sin[:].rearrange("p e h j -> p h j e"), op=ADD
            )

        def empty(engine, out, in_):
            if engine == "V":
                nc.vector.tensor_copy(out=out, in_=in_)
            else:
                nc.scalar.copy(out=out, in_=in_)

        gq_codes = {}
        gq_scales = {}

        def pack_tokens(t, r, engine="S"):
            gq_codes[t, r] = packed.tile(
                [P, UNIT_PASSES, P], U32, name="gq_codes%d%d" % (t, r), align_bytes=256
            )
            gq_scales[t, r] = packed.tile(
                [P, UNIT_PASSES, P], U8, name="gq_scales%d%d" % (t, r), align_bytes=256
            )
            words = g_tiles[t][:].bitcast(F32)
            bank = turned.tile([P, UNIT_PASSES, 2, P], F32, tag="bank")
            for j in range(UNIT_PASSES):
                for u in range(2):
                    first = (r * UNIT_PASSES + j) * PASS_WORDS + u * P
                    nc.tensor.transpose(bank[:, j, u, :], words[:, first : first + P], ident[:])
            grouped = stage.tile([P, UNIT_PASSES * 4 * P], BF16, tag="grouped_g", align_bytes=256)
            empty(
                engine,
                grouped[:].bitcast(F32).rearrange("p (j r u) -> p j r u", j=UNIT_PASSES, u=2),
                bank[:].rearrange("p j u r -> p j r u"),
            )
            nc.vector.quantize_mx(
                out=gq_codes[t, r][:].rearrange("p j r -> p (j r)").bitcast(E5M2_X4),
                scales=gq_scales[t, r][:].rearrange("p j r -> p (j r)"),
                in_=grouped[:],
            )

        w_codes = {}
        w_scales = {}

        turned_units = {}

        def turn_unit(n, j):
            turned_units[n, j] = blocks.tile([P, 2 * CHUNK], F32, name="turned_pass", align_bytes=256)
            nc.vector.transpose(
                out=turned_units[n, j][:],
                in_=w_units[n][:, 2 * j : 2 * j + 2].rearrange("p u i k -> p (u i k)").bitcast(F32),
            )

        def pack_unit(n, passes, engines="SSSS"):
            cr = UNIT_ORDER[n]
            if cr not in w_codes:
                w_codes[cr] = packed.tile(
                    [P, UNIT_PASSES, CHUNK], U32, name="w_codes%d" % n, align_bytes=256
                )
                w_scales[cr] = packed.tile(
                    [P, UNIT_PASSES, CHUNK], U8, name="w_scales%d" % n, align_bytes=256
                )
            for j in passes:
                grouped = stage.tile([P, 4 * CHUNK], BF16, tag="grouped_w", align_bytes=256)
                if n in TURNED_UNITS:
                    nc.scalar.copy(
                        out=grouped[:].bitcast(F32).rearrange("p (c u) -> p c u", u=2),
                        in_=turned_units[n, j][:].rearrange("p (u c) -> p c u", u=2),
                    )
                    nc.vector.quantize_mx(
                        out=w_codes[cr][:, j, :].bitcast(E4M3_X4),
                        scales=w_scales[cr][:, j, :],
                        in_=grouped[:],
                    )
                    continue
                words = w_units[n][:].bitcast(F32)
                for b in range(CHUNK // BANK_ROWS):
                    bank = turned.tile([P, 2, BANK_ROWS], F32, tag="bank")
                    for i in range(2):
                        for u in range(2):
                            first = j * PASS_WORDS + u * P
                            nc.tensor.transpose(
                                bank[:, u, i * P : (i + 1) * P],
                                words[:, 2 * b + i, first : first + P],
                                ident[:],
                            )
                    empty(
                        engines[2 * j + b],
                        grouped[:, b * 4 * BANK_ROWS : (b + 1) * 4 * BANK_ROWS]
                        .bitcast(F32)
                        .rearrange("p (r u) -> p r u", u=2),
                        bank[:].rearrange("p u r -> p r u"),
                    )
                nc.vector.quantize_mx(
                    out=w_codes[cr][:, j, :].bitcast(E4M3_X4),
                    scales=w_scales[cr][:, j, :],
                    in_=grouped[:],
                )

        def multiply(acc, t, c, r, j):
            nc.tensor.matmul_mx(
                out=acc[:],
                lhsT=gq_codes[t, r][:, j, :].bitcast(E5M2_X4),
                lhsT_scale=gq_scales[t, r][:, j, :],
                rhs=w_codes[c, r][:, j, :].bitcast(E4M3_X4),
                rhs_scale=w_scales[c, r][:, j, :],
                start=(r == 0 and j == 0),
                stop=(r == CHUNK_UNITS - 1 and j == UNIT_PASSES - 1),
            )

        def store(acc, t, c, engine):
            res = results.tile([P, CHUNK], F32, tag="res")
            pieces = LAST_PIECES if (c, t) == (CHUNKS - 1, TOKENS // P - 1) else 1
            step = CHUNK // pieces
            for d0 in range(0, CHUNK, step):
                empty(engine, res[:, d0 : d0 + step], acc[:, d0 : d0 + step])
                nc.sync.dma_start(
                    out=out_rows[t * P : (t + 1) * P, c * CHUNK + d0 : c * CHUNK + d0 + step],
                    in_=res[:, d0 : d0 + step],
                )

        open_groups = {}
        late = [(c, t, g) for c, t in LATE for g in range(PASSES)]

        def multiply_late(number):
            for c, t, g in late[:number]:
                if g == 0:
                    open_groups[c, t] = sums.tile([P, CHUNK], F32, name="grp", tag="accB")
                multiply(open_groups[c, t], t, c, g // UNIT_PASSES, g % UNIT_PASSES)
                if g == PASSES - 1:
                    store(open_groups[c, t], t, c, LATE_ENGINE.get((c, t), "S"))
            for i in range(min(number, len(late))):
                late.remove(late[0])

        for item in LOADS_FIRST:
            do_load(item)
        zeros = const.tile([P, CHUNK], BF16, name="zeros")
        nc.gpsimd.memset(zeros[:], 0.0)
        idle_sum = sums.tile([P, CHUNK], F32, name="idle_sum", tag="accB")

        def keep_awake(count):
            for i in range(count):
                nc.tensor.matmul(
                    out=idle_sum[:], lhsT=zeros[:, 0:P], rhs=zeros[:], start=True, stop=True
                )

        rotate(0, 0)
        rotate(1, 0)
        keep_awake(AWAKE_FIRST)
        pack_unit(0, (0,))
        keep_awake(AWAKE_BETWEEN)
        pack_unit(0, (1,))
        keep_awake(AWAKE_BETWEEN)
        pack_tokens(0, 0)
        pack_tokens(1, 0)
        keep_awake(AWAKE_BETWEEN)
        accs = {}
        for n in range(UNITS):
            c, r = UNIT_ORDER[n]
            for item in LOADS_ROUND.get(n, []):
                do_load(item)
            for piece in ROT_ROUND.get(n, []):
                rotate(*piece)
            if r == 0:
                for t in (0, 1):
                    accs[c, t] = sums.tile(
                        [P, CHUNK], F32, name="acc%d" % t, tag=ACC_TAG[c]
                    )
            for j in range(UNIT_PASSES):
                q = 2 * (n + 1) + j + TURN_LEAD
                if q // 2 in TURNED_UNITS:
                    turn_unit(q // 2, q % 2)
                if n + 1 < UNITS:
                    pack_unit(n + 1, (j,))
                for piece in TOK_HALF.get(2 * n + j, []):
                    pack_tokens(*piece)
                multiply_late(LATE_BEFORE.get(2 * n + j, 0))
                for t in (0, 1):
                    multiply(accs[c, t], t, c, r, j)
                multiply_late(LATE_AFTER.get(2 * n + j, 0))
            if r == CHUNK_UNITS - 1:
                for t in (0, 1):
                    store(accs[c, t], t, c, STORE_ENGINE[t])
        multiply_late(len(late))
